import numpy as np
import ml_dtypes

BF16 = ml_dtypes.bfloat16


def bf(x):
    return np.asarray(x, np.float32).astype(BF16)


def f32(x):
    return np.asarray(x, np.float32)


def f64(x):
    return np.asarray(x).astype(np.float64)


def striped(idx):
    return np.tile(idx.reshape(-1, 16).T, (8, 1))


C, S, H, K, N = 256, 256, 128, 4, 512
EPS = 1e-6


def setup_inputs():
    idx = np.concatenate([np.random.permutation(S)[:H] for _ in range(K)])
    return {"emb": f32(np.random.standard_normal((C, S))), "gain": f32(1.0 + 0.1 * np.random.standard_normal((C, 1))), "offs": striped(idx)}


def reference(emb, gain, offs):
    idx = offs[:16].T.reshape(-1)
    e = f64(emb)
    t = e / np.sqrt(np.mean(e * e, axis=0, keepdims=True) + EPS)
    return t[:, idx] * f64(gain)

@@ -1,0 +1,67 @@
+import concourse.mybir as mybir
+
+F32 = mybir.dt.float32
+BF16 = mybir.dt.bfloat16
+U16 = mybir.dt.uint16
+MULT = mybir.AluOpType.mult
+RSQRT = mybir.ActivationFunctionType.Abs_reciprocal_sqrt
+COPY = mybir.ActivationFunctionType.Copy
+
+P = 128
+C = 256
+S = 256
+N = 512
+EPS = 1e-6
+BLOCKS = C // P
+PIECE = S
+PIECES = N // PIECE
+
+FLOPS = 2 * C * S + C * S + C * N
+
+
+def tile_bitwhiskerlm_kernel(tc, emb, gain, offs, out):
+    nc = tc.nc
+    with (
+        tc.tile_pool(name="held", bufs=1) as held,
+        tc.psum_pool(name="psum", bufs=1) as psum,
+    ):
+        offsets = held.tile([P, N // 16], U16, name="offsets")
+        nc.sync.dma_start(offsets[:], offs)
+        emb_sb = [held.tile([P, S], F32, name=f"emb{b}") for b in range(BLOCKS)]
+        nc.sync.dma_start(emb_sb[0][:], emb[0:P, :])
+        nc.scalar.dma_start(emb_sb[1][:], emb[P : 2 * P, :])
+        gain_sb = [held.tile([P, 1], F32, name=f"gain{b}") for b in range(BLOCKS)]
+        for b in range(BLOCKS):
+            nc.scalar.dma_start(gain_sb[b][:], gain[b * P : (b + 1) * P, :])
+
+        ones = held.tile([P, P], BF16, name="ones")
+        nc.gpsimd.memset(ones[:], 1.0)
+        eps = held.tile([P, 1], F32, name="eps")
+        nc.gpsimd.memset(eps[:], EPS)
+
+        gain_wide = [held.tile([P, PIECE], F32, name=f"gain_wide{b}") for b in range(BLOCKS)]
+        for b in range(BLOCKS):
+            nc.scalar.activation(gain_wide[b][:], gain_sb[b][:].to_broadcast([P, PIECE]), COPY)
+
+        sums = psum.tile([P, S], F32, name="sums")
+        for b in range(BLOCKS):
+            squares = held.tile([P, S], BF16, name=f"squares{b}")
+            nc.vector.tensor_tensor(squares[:], emb_sb[b][:], emb_sb[b][:], MULT)
+            nc.tensor.matmul(sums[:], ones[:], squares[:], start=(b == 0), stop=(b == BLOCKS - 1))
+
+        rstd = held.tile([P, S], F32, name="rstd")
+        nc.scalar.activation(rstd[:], sums[:], RSQRT, bias=eps[:], scale=1.0 / C)
+
+        for b in range(BLOCKS):
+            table = held.tile([P, S], F32, name=f"table{b}")
+            nc.vector.tensor_tensor(table[:], emb_sb[b][:], rstd[:], MULT)
+            for k in range(PIECES):
+                picked = held.tile([P, PIECE], F32, name=f"picked{b}{k}")
+                nc.vector.tensor_tensor(
+                    picked[:],
+                    table[:].indirect(offsets[:, k * (PIECE // 16) : (k + 1) * (PIECE // 16)]),
+                    gain_wide[b][:],
+                    MULT,
+                )
+                queue = nc.sync if k % 2 == 0 else nc.scalar
+                queue.dma_start(out[b * P : (b + 1) * P, k * PIECE : (k + 1) * PIECE], picked[:])

@@ -39,6 +39,9 @@ def tile_bitwhiskerlm_kernel(tc, emb, gain, offs, out):
         eps = held.tile([P, 1], F32, name="eps")
         nc.gpsimd.memset(eps[:], EPS)
 
+        warm = held.tile([P, 1], F32, name="warm")
+        nc.scalar.activation(warm[:], eps[:], RSQRT)
+
         gain_wide = [held.tile([P, PIECE], F32, name=f"gain_wide{b}") for b in range(BLOCKS)]
         for b in range(BLOCKS):
             nc.scalar.activation(gain_wide[b][:], gain_sb[b][:].to_broadcast([P, PIECE]), COPY)

@@ -5,7 +5,6 @@ BF16 = mybir.dt.bfloat16
 U16 = mybir.dt.uint16
 MULT = mybir.AluOpType.mult
 RSQRT = mybir.ActivationFunctionType.Abs_reciprocal_sqrt
-COPY = mybir.ActivationFunctionType.Copy
 
 P = 128
 C = 256
@@ -15,6 +14,8 @@ EPS = 1e-6
 BLOCKS = C // P
 PIECE = S
 PIECES = N // PIECE
+HALVES = 2
+HALF = S // HALVES
 
 FLOPS = 2 * C * S + C * S + C * N
 
@@ -25,11 +26,13 @@ def tile_bitwhiskerlm_kernel(tc, emb, gain, offs, out):
         tc.tile_pool(name="held", bufs=1) as held,
         tc.psum_pool(name="psum", bufs=1) as psum,
     ):
+        emb_sb = [held.tile([P, S], F32, name=f"emb{b}") for b in range(BLOCKS)]
+        for h in range(HALVES):
+            cols = slice(h * HALF, (h + 1) * HALF)
+            nc.sync.dma_start(emb_sb[0][:, cols], emb[0:P, cols])
+            nc.scalar.dma_start(emb_sb[1][:, cols], emb[P : 2 * P, cols])
         offsets = held.tile([P, N // 16], U16, name="offsets")
         nc.sync.dma_start(offsets[:], offs)
-        emb_sb = [held.tile([P, S], F32, name=f"emb{b}") for b in range(BLOCKS)]
-        nc.sync.dma_start(emb_sb[0][:], emb[0:P, :])
-        nc.scalar.dma_start(emb_sb[1][:], emb[P : 2 * P, :])
         gain_sb = [held.tile([P, 1], F32, name=f"gain{b}") for b in range(BLOCKS)]
         for b in range(BLOCKS):
             nc.scalar.dma_start(gain_sb[b][:], gain[b * P : (b + 1) * P, :])
@@ -44,20 +47,23 @@ def tile_bitwhiskerlm_kernel(tc, emb, gain, offs, out):
 
         gain_wide = [held.tile([P, PIECE], F32, name=f"gain_wide{b}") for b in range(BLOCKS)]
         for b in range(BLOCKS):
-            nc.scalar.activation(gain_wide[b][:], gain_sb[b][:].to_broadcast([P, PIECE]), COPY)
-
-        sums = psum.tile([P, S], F32, name="sums")
-        for b in range(BLOCKS):
-            squares = held.tile([P, S], BF16, name=f"squares{b}")
-            nc.vector.tensor_tensor(squares[:], emb_sb[b][:], emb_sb[b][:], MULT)
-            nc.tensor.matmul(sums[:], ones[:], squares[:], start=(b == 0), stop=(b == BLOCKS - 1))
+            nc.gpsimd.tensor_copy(gain_wide[b][:], gain_sb[b][:].to_broadcast([P, PIECE]))
 
         rstd = held.tile([P, S], F32, name="rstd")
-        nc.scalar.activation(rstd[:], sums[:], RSQRT, bias=eps[:], scale=1.0 / C)
+        for h in range(HALVES):
+            cols = slice(h * HALF, (h + 1) * HALF)
+            sums = psum.tile([P, HALF], F32, name=f"sums{h}")
+            for b in range(BLOCKS):
+                squares = held.tile([P, HALF], BF16, name=f"squares{b}{h}")
+                nc.vector.tensor_tensor(squares[:], emb_sb[b][:, cols], emb_sb[b][:, cols], MULT)
+                nc.tensor.matmul(sums[:], ones[:], squares[:], start=(b == 0), stop=(b == BLOCKS - 1))
+            nc.scalar.activation(rstd[:, cols], sums[:], RSQRT, bias=eps[:], scale=1.0 / C)
 
         for b in range(BLOCKS):
             table = held.tile([P, S], F32, name=f"table{b}")
-            nc.vector.tensor_tensor(table[:], emb_sb[b][:], rstd[:], MULT)
+            for h in range(HALVES):
+                cols = slice(h * HALF, (h + 1) * HALF)
+                nc.vector.tensor_tensor(table[:, cols], emb_sb[b][:, cols], rstd[:, cols], MULT)
             for k in range(PIECES):
                 picked = held.tile([P, PIECE], F32, name=f"picked{b}{k}")
                 nc.vector.tensor_tensor(

@@ -63,7 +63,8 @@ def tile_bitwhiskerlm_kernel(tc, emb, gain, offs, out):
             table = held.tile([P, S], F32, name=f"table{b}")
             for h in range(HALVES):
                 cols = slice(h * HALF, (h + 1) * HALF)
-                nc.vector.tensor_tensor(table[:, cols], emb_sb[b][:, cols], rstd[:, cols], MULT)
+                engine = nc.vector if b == 0 else nc.gpsimd
+                engine.tensor_tensor(table[:, cols], emb_sb[b][:, cols], rstd[:, cols], MULT)
             for k in range(PIECES):
                 picked = held.tile([P, PIECE], F32, name=f"picked{b}{k}")
                 nc.vector.tensor_tensor(

@@ -5,6 +5,7 @@ BF16 = mybir.dt.bfloat16
 U16 = mybir.dt.uint16
 MULT = mybir.AluOpType.mult
 RSQRT = mybir.ActivationFunctionType.Abs_reciprocal_sqrt
+COPY = mybir.ActivationFunctionType.Copy
 
 P = 128
 C = 256
@@ -45,10 +46,6 @@ def tile_bitwhiskerlm_kernel(tc, emb, gain, offs, out):
         warm = held.tile([P, 1], F32, name="warm")
         nc.scalar.activation(warm[:], eps[:], RSQRT)
 
-        gain_wide = [held.tile([P, PIECE], F32, name=f"gain_wide{b}") for b in range(BLOCKS)]
-        for b in range(BLOCKS):
-            nc.gpsimd.tensor_copy(gain_wide[b][:], gain_sb[b][:].to_broadcast([P, PIECE]))
-
         rstd = held.tile([P, S], F32, name="rstd")
         for h in range(HALVES):
             cols = slice(h * HALF, (h + 1) * HALF)
@@ -59,12 +56,15 @@ def tile_bitwhiskerlm_kernel(tc, emb, gain, offs, out):
                 nc.tensor.matmul(sums[:], ones[:], squares[:], start=(b == 0), stop=(b == BLOCKS - 1))
             nc.scalar.activation(rstd[:, cols], sums[:], RSQRT, bias=eps[:], scale=1.0 / C)
 
+        gain_wide = [held.tile([P, PIECE], F32, name=f"gain_wide{b}") for b in range(BLOCKS)]
+        nc.vector.tensor_copy(gain_wide[0][:], gain_sb[0][:].to_broadcast([P, PIECE]))
+        nc.scalar.activation(gain_wide[1][:], gain_sb[1][:].to_broadcast([P, PIECE]), COPY)
+
         for b in range(BLOCKS):
             table = held.tile([P, S], F32, name=f"table{b}")
             for h in range(HALVES):
                 cols = slice(h * HALF, (h + 1) * HALF)
-                engine = nc.vector if b == 0 else nc.gpsimd
-                engine.tensor_tensor(table[:, cols], emb_sb[b][:, cols], rstd[:, cols], MULT)
+                nc.vector.tensor_tensor(table[:, cols], emb_sb[b][:, cols], rstd[:, cols], MULT)
             for k in range(PIECES):
                 picked = held.tile([P, PIECE], F32, name=f"picked{b}{k}")
                 nc.vector.tensor_tensor(

@@ -14,7 +14,9 @@ N = 512
 EPS = 1e-6
 BLOCKS = C // P
 PIECE = S
-PIECES = N // PIECE
+WIDTHS_PLAIN = (PIECE, PIECE)
+WIDTHS_LAST = (PIECE, PIECE // 2, PIECE // 4, PIECE // 4)
+assert sum(WIDTHS_PLAIN) == N and sum(WIDTHS_LAST) == N
 HALVES = 2
 HALF = S // HALVES
 
@@ -65,13 +67,15 @@ def tile_bitwhiskerlm_kernel(tc, emb, gain, offs, out):
             for h in range(HALVES):
                 cols = slice(h * HALF, (h + 1) * HALF)
                 nc.vector.tensor_tensor(table[:, cols], emb_sb[b][:, cols], rstd[:, cols], MULT)
-            for k in range(PIECES):
-                picked = held.tile([P, PIECE], F32, name=f"picked{b}{k}")
+            first = 0
+            for k, width in enumerate(WIDTHS_LAST if b == BLOCKS - 1 else WIDTHS_PLAIN):
+                picked = held.tile([P, width], F32, name=f"picked{b}{k}")
                 nc.vector.tensor_tensor(
                     picked[:],
-                    table[:].indirect(offsets[:, k * (PIECE // 16) : (k + 1) * (PIECE // 16)]),
-                    gain_wide[b][:],
+                    table[:].indirect(offsets[:, first // 16 : (first + width) // 16]),
+                    gain_wide[b][:, :width],
                     MULT,
                 )
                 queue = nc.sync if k % 2 == 0 else nc.scalar
-                queue.dma_start(out[b * P : (b + 1) * P, k * PIECE : (k + 1) * PIECE], picked[:])
+                queue.dma_start(out[b * P : (b + 1) * P, first : first + width], picked[:])
+                first += width

@@ -19,6 +19,8 @@ WIDTHS_LAST = (PIECE, PIECE // 2, PIECE // 4, PIECE // 4)
 assert sum(WIDTHS_PLAIN) == N and sum(WIDTHS_LAST) == N
 HALVES = 2
 HALF = S // HALVES
+PARTS = 4
+PART = S // PARTS
 
 FLOPS = 2 * C * S + C * S + C * N
 
@@ -49,11 +51,11 @@ def tile_bitwhiskerlm_kernel(tc, emb, gain, offs, out):
         nc.scalar.activation(warm[:], eps[:], RSQRT)
 
         rstd = held.tile([P, S], F32, name="rstd")
-        for h in range(HALVES):
-            cols = slice(h * HALF, (h + 1) * HALF)
-            sums = psum.tile([P, HALF], F32, name=f"sums{h}")
+        for h in range(PARTS):
+            cols = slice(h * PART, (h + 1) * PART)
+            sums = psum.tile([P, PART], F32, name=f"sums{h}")
             for b in range(BLOCKS):
-                squares = held.tile([P, HALF], BF16, name=f"squares{b}{h}")
+                squares = held.tile([P, PART], BF16, name=f"squares{b}{h}")
                 nc.vector.tensor_tensor(squares[:], emb_sb[b][:, cols], emb_sb[b][:, cols], MULT)
                 nc.tensor.matmul(sums[:], ones[:], squares[:], start=(b == 0), stop=(b == BLOCKS - 1))
             nc.scalar.activation(rstd[:, cols], sums[:], RSQRT, bias=eps[:], scale=1.0 / C)
@@ -64,8 +66,8 @@ def tile_bitwhiskerlm_kernel(tc, emb, gain, offs, out):
 
         for b in range(BLOCKS):
             table = held.tile([P, S], F32, name=f"table{b}")
-            for h in range(HALVES):
-                cols = slice(h * HALF, (h + 1) * HALF)
+            for h in range(PARTS):
+                cols = slice(h * PART, (h + 1) * PART)
                 nc.vector.tensor_tensor(table[:, cols], emb_sb[b][:, cols], rstd[:, cols], MULT)
             first = 0
             for k, width in enumerate(WIDTHS_LAST if b == BLOCKS - 1 else WIDTHS_PLAIN):

@@ -66,8 +66,9 @@ def tile_bitwhiskerlm_kernel(tc, emb, gain, offs, out):
 
         for b in range(BLOCKS):
             table = held.tile([P, S], F32, name=f"table{b}")
-            for h in range(PARTS):
-                cols = slice(h * PART, (h + 1) * PART)
+            t_parts = PARTS if b == 0 else 1
+            for h in range(t_parts):
+                cols = slice(h * (S // t_parts), (h + 1) * (S // t_parts))
                 nc.vector.tensor_tensor(table[:, cols], emb_sb[b][:, cols], rstd[:, cols], MULT)
             first = 0
             for k, width in enumerate(WIDTHS_LAST if b == BLOCKS - 1 else WIDTHS_PLAIN):

@@ -15,7 +15,7 @@ EPS = 1e-6
 BLOCKS = C // P
 PIECE = S
 WIDTHS_PLAIN = (PIECE, PIECE)
-WIDTHS_LAST = (PIECE, PIECE // 2, PIECE // 4, PIECE // 4)
+WIDTHS_LAST = (PIECE, PIECE // 2, PIECE // 2)
 assert sum(WIDTHS_PLAIN) == N and sum(WIDTHS_LAST) == N
 HALVES = 2
 HALF = S // HALVES

@@ -5,7 +5,6 @@ BF16 = mybir.dt.bfloat16
 U16 = mybir.dt.uint16
 MULT = mybir.AluOpType.mult
 RSQRT = mybir.ActivationFunctionType.Abs_reciprocal_sqrt
-COPY = mybir.ActivationFunctionType.Copy
 
 P = 128
 C = 256
@@ -61,8 +60,8 @@ def tile_bitwhiskerlm_kernel(tc, emb, gain, offs, out):
             nc.scalar.activation(rstd[:, cols], sums[:], RSQRT, bias=eps[:], scale=1.0 / C)
 
         gain_wide = [held.tile([P, PIECE], F32, name=f"gain_wide{b}") for b in range(BLOCKS)]
-        nc.vector.tensor_copy(gain_wide[0][:], gain_sb[0][:].to_broadcast([P, PIECE]))
-        nc.scalar.activation(gain_wide[1][:], gain_sb[1][:].to_broadcast([P, PIECE]), COPY)
+        for b in range(BLOCKS):
+            nc.vector.tensor_copy(gain_wide[b][:], gain_sb[b][:].to_broadcast([P, PIECE]))
 
         for b in range(BLOCKS):
             table = held.tile([P, S], F32, name=f"table{b}")

@@ -18,8 +18,10 @@ WIDTHS_LAST = (PIECE, PIECE // 2, PIECE // 2)
 assert sum(WIDTHS_PLAIN) == N and sum(WIDTHS_LAST) == N
 HALVES = 2
 HALF = S // HALVES
-PARTS = 4
-PART = S // PARTS
+PART = S // 4
+PART_WIDTHS = (PART, PART, PART, PART // 2, PART // 2)
+assert sum(PART_WIDTHS) == S
+PART_COLS = [slice(sum(PART_WIDTHS[:h]), sum(PART_WIDTHS[: h + 1])) for h in range(len(PART_WIDTHS))]
 
 FLOPS = 2 * C * S + C * S + C * N
 
@@ -50,11 +52,10 @@ def tile_bitwhiskerlm_kernel(tc, emb, gain, offs, out):
         nc.scalar.activation(warm[:], eps[:], RSQRT)
 
         rstd = held.tile([P, S], F32, name="rstd")
-        for h in range(PARTS):
-            cols = slice(h * PART, (h + 1) * PART)
-            sums = psum.tile([P, PART], F32, name=f"sums{h}")
+        for h, cols in enumerate(PART_COLS):
+            sums = psum.tile([P, PART_WIDTHS[h]], F32, name=f"sums{h}")
             for b in range(BLOCKS):
-                squares = held.tile([P, PART], BF16, name=f"squares{b}{h}")
+                squares = held.tile([P, PART_WIDTHS[h]], BF16, name=f"squares{b}{h}")
                 nc.vector.tensor_tensor(squares[:], emb_sb[b][:, cols], emb_sb[b][:, cols], MULT)
                 nc.tensor.matmul(sums[:], ones[:], squares[:], start=(b == 0), stop=(b == BLOCKS - 1))
             nc.scalar.activation(rstd[:, cols], sums[:], RSQRT, bias=eps[:], scale=1.0 / C)
@@ -65,9 +66,7 @@ def tile_bitwhiskerlm_kernel(tc, emb, gain, offs, out):
 
         for b in range(BLOCKS):
             table = held.tile([P, S], F32, name=f"table{b}")
-            t_parts = PARTS if b == 0 else 1
-            for h in range(t_parts):
-                cols = slice(h * (S // t_parts), (h + 1) * (S // t_parts))
+            for cols in PART_COLS if b == 0 else (slice(0, S),):
                 nc.vector.tensor_tensor(table[:, cols], emb_sb[b][:, cols], rstd[:, cols], MULT)
             first = 0
             for k, width in enumerate(WIDTHS_LAST if b == BLOCKS - 1 else WIDTHS_PLAIN):

@@ -32,16 +32,17 @@ def tile_bitwhiskerlm_kernel(tc, emb, gain, offs, out):
         tc.tile_pool(name="held", bufs=1) as held,
         tc.psum_pool(name="psum", bufs=1) as psum,
     ):
+        emb_rows = emb.rearrange("(p b) s -> p b s", b=BLOCKS)
+        out_rows = out.rearrange("(p b) n -> p b n", b=BLOCKS)
         emb_sb = [held.tile([P, S], F32, name=f"emb{b}") for b in range(BLOCKS)]
         for h in range(HALVES):
             cols = slice(h * HALF, (h + 1) * HALF)
-            nc.sync.dma_start(emb_sb[0][:, cols], emb[0:P, cols])
-            nc.scalar.dma_start(emb_sb[1][:, cols], emb[P : 2 * P, cols])
+            nc.sync.dma_start(emb_sb[0][:, cols], emb_rows[:, 0, cols])
+            nc.scalar.dma_start(emb_sb[1][:, cols], emb_rows[:, 1, cols])
         offsets = held.tile([P, N // 16], U16, name="offsets")
         nc.sync.dma_start(offsets[:], offs)
-        gain_sb = [held.tile([P, 1], F32, name=f"gain{b}") for b in range(BLOCKS)]
-        for b in range(BLOCKS):
-            nc.scalar.dma_start(gain_sb[b][:], gain[b * P : (b + 1) * P, :])
+        gain_sb = held.tile([P, BLOCKS], F32, name="gain_sb")
+        nc.scalar.dma_start(gain_sb[:], gain.rearrange("(p b) o -> p (b o)", b=BLOCKS))
 
         ones = held.tile([P, P], BF16, name="ones")
         nc.gpsimd.memset(ones[:], 1.0)
@@ -62,7 +63,7 @@ def tile_bitwhiskerlm_kernel(tc, emb, gain, offs, out):
 
         gain_wide = [held.tile([P, PIECE], F32, name=f"gain_wide{b}") for b in range(BLOCKS)]
         for b in range(BLOCKS):
-            nc.vector.tensor_copy(gain_wide[b][:], gain_sb[b][:].to_broadcast([P, PIECE]))
+            nc.vector.tensor_copy(gain_wide[b][:], gain_sb[:, b : b + 1].to_broadcast([P, PIECE]))
 
         for b in range(BLOCKS):
             table = held.tile([P, S], F32, name=f"table{b}")
@@ -78,5 +79,5 @@ def tile_bitwhiskerlm_kernel(tc, emb, gain, offs, out):
                     MULT,
                 )
                 queue = nc.sync if k % 2 == 0 else nc.scalar
-                queue.dma_start(out[b * P : (b + 1) * P, first : first + width], picked[:])
+                queue.dma_start(out_rows[:, b, first : first + width], picked[:])
                 first += width

@@ -13,9 +13,8 @@ N = 512
 EPS = 1e-6
 BLOCKS = C // P
 PIECE = S
-WIDTHS_PLAIN = (PIECE, PIECE)
-WIDTHS_LAST = (PIECE, PIECE // 2, PIECE // 2)
-assert sum(WIDTHS_PLAIN) == N and sum(WIDTHS_LAST) == N
+WIDTHS = (PIECE, PIECE // 2, PIECE // 2)
+assert sum(WIDTHS) == N
 HALVES = 2
 HALF = S // HALVES
 PART = S // 4
@@ -70,7 +69,7 @@ def tile_bitwhiskerlm_kernel(tc, emb, gain, offs, out):
             for cols in PART_COLS if b == 0 else (slice(0, S),):
                 nc.vector.tensor_tensor(table[:, cols], emb_sb[b][:, cols], rstd[:, cols], MULT)
             first = 0
-            for k, width in enumerate(WIDTHS_LAST if b == BLOCKS - 1 else WIDTHS_PLAIN):
+            for k, width in enumerate(WIDTHS):
                 picked = held.tile([P, width], F32, name=f"picked{b}{k}")
                 nc.vector.tensor_tensor(
                     picked[:],
@@ -78,6 +77,6 @@ def tile_bitwhiskerlm_kernel(tc, emb, gain, offs, out):
                     gain_wide[b][:, :width],
                     MULT,
                 )
-                queue = nc.sync if k % 2 == 0 else nc.scalar
+                queue = nc.scalar if (b * len(WIDTHS) + k) % 2 == 0 else nc.sync
                 queue.dma_start(out_rows[:, b, first : first + width], picked[:])
                 first += width

@@ -13,8 +13,10 @@ N = 512
 EPS = 1e-6
 BLOCKS = C // P
 PIECE = S
-WIDTHS = (PIECE, PIECE // 2, PIECE // 2)
-assert sum(WIDTHS) == N
+WIDTHS_PLAIN = (PIECE, PIECE)
+WIDTHS_LAST = (PIECE, PIECE // 2, PIECE // 4, PIECE // 4)
+assert sum(WIDTHS_PLAIN) == N and sum(WIDTHS_LAST) == N
+WIDTHS = [WIDTHS_PLAIN] * (BLOCKS - 1) + [WIDTHS_LAST]
 HALVES = 2
 HALF = S // HALVES
 PART = S // 4
@@ -69,7 +71,7 @@ def tile_bitwhiskerlm_kernel(tc, emb, gain, offs, out):
             for cols in PART_COLS if b == 0 else (slice(0, S),):
                 nc.vector.tensor_tensor(table[:, cols], emb_sb[b][:, cols], rstd[:, cols], MULT)
             first = 0
-            for k, width in enumerate(WIDTHS):
+            for k, width in enumerate(WIDTHS[b]):
                 picked = held.tile([P, width], F32, name=f"picked{b}{k}")
                 nc.vector.tensor_tensor(
                     picked[:],
@@ -77,6 +79,6 @@ def tile_bitwhiskerlm_kernel(tc, emb, gain, offs, out):
                     gain_wide[b][:, :width],
                     MULT,
                 )
-                queue = nc.scalar if (b * len(WIDTHS) + k) % 2 == 0 else nc.sync
+                queue = nc.scalar if k % 2 == 0 else nc.sync
                 queue.dma_start(out_rows[:, b, first : first + width], picked[:])
                 first += width

@@ -14,7 +14,7 @@ EPS = 1e-6
 BLOCKS = C // P
 PIECE = S
 WIDTHS_PLAIN = (PIECE, PIECE)
-WIDTHS_LAST = (PIECE, PIECE // 2, PIECE // 4, PIECE // 4)
+WIDTHS_LAST = (PIECE, PIECE // 2, PIECE // 2)
 assert sum(WIDTHS_PLAIN) == N and sum(WIDTHS_LAST) == N
 WIDTHS = [WIDTHS_PLAIN] * (BLOCKS - 1) + [WIDTHS_LAST]
 HALVES = 2
@@ -35,11 +35,10 @@ def tile_bitwhiskerlm_kernel(tc, emb, gain, offs, out):
     ):
         emb_rows = emb.rearrange("(p b) s -> p b s", b=BLOCKS)
         out_rows = out.rearrange("(p b) n -> p b n", b=BLOCKS)
-        emb_sb = [held.tile([P, S], F32, name=f"emb{b}") for b in range(BLOCKS)]
-        for h in range(HALVES):
+        emb_sb = held.tile([P, BLOCKS, S], F32, name="emb_sb")
+        for h, queue in enumerate((nc.sync, nc.scalar)):
             cols = slice(h * HALF, (h + 1) * HALF)
-            nc.sync.dma_start(emb_sb[0][:, cols], emb_rows[:, 0, cols])
-            nc.scalar.dma_start(emb_sb[1][:, cols], emb_rows[:, 1, cols])
+            queue.dma_start(emb_sb[:, :, cols], emb_rows[:, :, cols])
         offsets = held.tile([P, N // 16], U16, name="offsets")
         nc.sync.dma_start(offsets[:], offs)
         gain_sb = held.tile([P, BLOCKS], F32, name="gain_sb")
@@ -58,7 +57,7 @@ def tile_bitwhiskerlm_kernel(tc, emb, gain, offs, out):
             sums = psum.tile([P, PART_WIDTHS[h]], F32, name=f"sums{h}")
             for b in range(BLOCKS):
                 squares = held.tile([P, PART_WIDTHS[h]], BF16, name=f"squares{b}{h}")
-                nc.vector.tensor_tensor(squares[:], emb_sb[b][:, cols], emb_sb[b][:, cols], MULT)
+                nc.vector.tensor_tensor(squares[:], emb_sb[:, b, cols], emb_sb[:, b, cols], MULT)
                 nc.tensor.matmul(sums[:], ones[:], squares[:], start=(b == 0), stop=(b == BLOCKS - 1))
             nc.scalar.activation(rstd[:, cols], sums[:], RSQRT, bias=eps[:], scale=1.0 / C)
 
@@ -69,16 +68,19 @@ def tile_bitwhiskerlm_kernel(tc, emb, gain, offs, out):
         for b in range(BLOCKS):
             table = held.tile([P, S], F32, name=f"table{b}")
             for cols in PART_COLS if b == 0 else (slice(0, S),):
-                nc.vector.tensor_tensor(table[:, cols], emb_sb[b][:, cols], rstd[:, cols], MULT)
+                nc.vector.tensor_tensor(table[:, cols], emb_sb[:, b, cols], rstd[:, cols], MULT)
+            picked = held.tile([P, N], F32, name=f"picked{b}")
             first = 0
             for k, width in enumerate(WIDTHS[b]):
-                picked = held.tile([P, width], F32, name=f"picked{b}{k}")
                 nc.vector.tensor_tensor(
-                    picked[:],
+                    picked[:, first : first + width],
                     table[:].indirect(offsets[:, first // 16 : (first + width) // 16]),
                     gain_wide[b][:, :width],
                     MULT,
                 )
-                queue = nc.scalar if k % 2 == 0 else nc.sync
-                queue.dma_start(out_rows[:, b, first : first + width], picked[:])
+                if b == BLOCKS - 1:
+                    queue = nc.scalar if k == 1 else nc.sync
+                    queue.dma_start(out_rows[:, b, first : first + width], picked[:, first : first + width])
                 first += width
+            if b < BLOCKS - 1:
+                nc.scalar.dma_start(out_rows[:, b, :], picked[:])

import concourse.mybir as mybir

F32 = mybir.dt.float32
BF16 = mybir.dt.bfloat16
U16 = mybir.dt.uint16
MULT = mybir.AluOpType.mult
RSQRT = mybir.ActivationFunctionType.Abs_reciprocal_sqrt

P = 128
C = 256
S = 256
N = 512
EPS = 1e-6
BLOCKS = C // P
PIECE = S
WIDTHS_PLAIN = (PIECE, PIECE)
WIDTHS_LAST = (PIECE, PIECE // 2, PIECE // 2)
assert sum(WIDTHS_PLAIN) == N and sum(WIDTHS_LAST) == N
WIDTHS = [WIDTHS_PLAIN] * (BLOCKS - 1) + [WIDTHS_LAST]
HALVES = 2
HALF = S // HALVES
PART = S // 4
PART_WIDTHS = (PART, PART, PART, PART // 2, PART // 2)
assert sum(PART_WIDTHS) == S
PART_COLS = [slice(sum(PART_WIDTHS[:h]), sum(PART_WIDTHS[: h + 1])) for h in range(len(PART_WIDTHS))]

FLOPS = 2 * C * S + C * S + C * N


def tile_bitwhiskerlm_kernel(tc, emb, gain, offs, out):
    nc = tc.nc
    with (
        tc.tile_pool(name="held", bufs=1) as held,
        tc.psum_pool(name="psum", bufs=1) as psum,
    ):
        emb_rows = emb.rearrange("(p b) s -> p b s", b=BLOCKS)
        out_rows = out.rearrange("(p b) n -> p b n", b=BLOCKS)
        emb_sb = held.tile([P, BLOCKS, S], F32, name="emb_sb")
        for h, queue in enumerate((nc.sync, nc.scalar)):
            cols = slice(h * HALF, (h + 1) * HALF)
            queue.dma_start(emb_sb[:, :, cols], emb_rows[:, :, cols])
        offsets = held.tile([P, N // 16], U16, name="offsets")
        nc.sync.dma_start(offsets[:], offs)
        gain_sb = held.tile([P, BLOCKS], F32, name="gain_sb")
        nc.scalar.dma_start(gain_sb[:], gain.rearrange("(p b) o -> p (b o)", b=BLOCKS))

        ones = held.tile([P, P], BF16, name="ones")
        nc.gpsimd.memset(ones[:], 1.0)
        eps = held.tile([P, 1], F32, name="eps")
        nc.gpsimd.memset(eps[:], EPS)

        warm = held.tile([P, 1], F32, name="warm")
        nc.scalar.activation(warm[:], eps[:], RSQRT)

        rstd = held.tile([P, S], F32, name="rstd")
        for h, cols in enumerate(PART_COLS):
            sums = psum.tile([P, PART_WIDTHS[h]], F32, name=f"sums{h}")
            for b in range(BLOCKS):
                squares = held.tile([P, PART_WIDTHS[h]], BF16, name=f"squares{b}{h}")
                nc.vector.tensor_tensor(squares[:], emb_sb[:, b, cols], emb_sb[:, b, cols], MULT)
                nc.tensor.matmul(sums[:], ones[:], squares[:], start=(b == 0), stop=(b == BLOCKS - 1))
            nc.scalar.activation(rstd[:, cols], sums[:], RSQRT, bias=eps[:], scale=1.0 / C)

        gain_wide = [held.tile([P, PIECE], F32, name=f"gain_wide{b}") for b in range(BLOCKS)]
        for b in range(BLOCKS):
            nc.vector.tensor_copy(gain_wide[b][:], gain_sb[:, b : b + 1].to_broadcast([P, PIECE]))

        for b in range(BLOCKS):
            table = held.tile([P, S], F32, name=f"table{b}")
            for cols in PART_COLS if b == 0 else (slice(0, S),):
                nc.vector.tensor_tensor(table[:, cols], emb_sb[:, b, cols], rstd[:, cols], MULT)
            picked = held.tile([P, N], F32, name=f"picked{b}")
            first = 0
            for k, width in enumerate(WIDTHS[b]):
                nc.vector.tensor_tensor(
                    picked[:, first : first + width],
                    table[:].indirect(offsets[:, first // 16 : (first + width) // 16]),
                    gain_wide[b][:, :width],
                    MULT,
                )
                if b == BLOCKS - 1:
                    queue = nc.scalar if k == 1 else nc.sync
                    queue.dma_start(out_rows[:, b, first : first + width], picked[:, first : first + width])
                first += width
            if b < BLOCKS - 1:
                nc.scalar.dma_start(out_rows[:, b, :], picked[:])
